import numpy as np
import ml_dtypes


def mxq(x, axis, fmt="e4m3"):
    dtype, down = {"e4m3": (ml_dtypes.float8_e4m3fn, 7), "e5m2": (ml_dtypes.float8_e5m2, 14)}[fmt]
    v = np.moveaxis(np.asarray(x, np.float32).astype(ml_dtypes.bfloat16).astype(np.float64), axis, -1)
    blocks = v.reshape(v.shape[:-1] + (-1, 32))
    amax = np.abs(blocks).max(-1, keepdims=True)
    byte = np.maximum(np.where(amax > 0, np.frexp(amax)[1] - 1 + 127, 0) - down, 1)
    scale = np.exp2(byte - 127.0)
    codes = (blocks / scale).astype(np.float32).astype(dtype).astype(np.float64)
    return np.moveaxis((codes * scale).reshape(v.shape), -1, axis)


WIDE = False


def mx_kscale(k):
    if not WIDE:
        return np.ones(k)
    levels = np.array([10, -10, 5, -5, 0])
    a = np.random.permutation(np.resize(levels, k // 512 * 4)).reshape(k // 512, 4)
    idx = np.arange(k)
    return np.exp2(a[idx // 512, idx % 128 // 32])


BF16 = ml_dtypes.bfloat16


def bf(x):
    return np.asarray(x, np.float32).astype(BF16)


def f64(x):
    return np.asarray(x).astype(np.float64)


T, B, D, M = 128, 32, 1024, 512
TEMP = 0.1
QS = 0.3
SC = 2.0
MS = SC * TEMP / (QS * np.sqrt(D))
WS = QS * np.sqrt(SC**2 / D + 0.4 / B)


def sigmoid(v):
    return 1.0 / (1.0 + np.exp(-v))


def setup_inputs():
    s = mx_kscale(D)
    return {"queries": bf(np.random.standard_normal((T, B, D)) * QS / s),
            "memory_items": bf(np.random.standard_normal((M, D)) * MS * s),
            "wq": bf(np.random.standard_normal((M, D)) * WS * s),
            "U_w": bf(np.random.standard_normal((D, D)) / (MS * np.sqrt(D)) / s[None, :]),
            "W_w": bf(np.random.standard_normal((D, D)) / (WS * np.sqrt(D)) / s[None, :])}


def reference(queries, memory_items, wq, U_w, W_w):
    q = f64(queries).reshape(T * B, D)
    mem = f64(memory_items)
    w = f64(wq)
    gate = sigmoid((mxq(mem, 1, "e4m3") @ mxq(f64(U_w), 1, "e4m3").T) + (mxq(w, 1, "e4m3") @ mxq(f64(W_w), 1, "e4m3").T))
    m_new = (1.0 - gate) * mem + gate * w
    logits = (mxq(q, 1, "e4m3") @ mxq(m_new, 1, "e4m3").T) / TEMP
    e = np.exp(logits - logits.max(-1, keepdims=True))
    w_att = e / e.sum(-1, keepdims=True)
    return m_new, w_att.reshape(T, B, M)

@@ -1,0 +1,221 @@
+from contextlib import ExitStack
+
+import concourse.mybir as mybir
+from concourse.masks import make_identity
+
+F32 = mybir.dt.float32
+BF16 = mybir.dt.bfloat16
+U32 = mybir.dt.uint32
+U8 = mybir.dt.uint8
+FP8X4 = mybir.dt.float8_e4m3fn_x4
+ACT = mybir.ActivationFunctionType
+AXIS = mybir.AxisListType
+
+P = 128
+FEATURES = 1024
+SLOTS = 512
+BATCH = 32
+TEMPERATURE = 0.1
+PACK = 4
+K_PASS = P * PACK
+PASSES = FEATURES // K_PASS
+TILES = 4
+CHUNK_ROWS = TILES * P
+CHUNK_WORDS = CHUNK_ROWS * PASSES
+HALVES = FEATURES // CHUNK_ROWS
+QUERY_CHUNKS = BATCH // TILES
+QUERY_BUFFERS = 4
+AHEAD = 2
+
+FLOPS = 2 * (2 * SLOTS * FEATURES * FEATURES) + 2 * (P * BATCH) * SLOTS * FEATURES
+
+
+def stationary_cols(n, g):
+    return slice((n * PASSES + g) * P, (n * PASSES + g + 1) * P)
+
+
+def moving_cols(g):
+    return slice(g * CHUNK_ROWS, (g + 1) * CHUNK_ROWS)
+
+
+def tile_gatedmemorymodule_pb_t_kernel(tc, queries, memory_items, wq, U_w, W_w, out_0, out_1):
+    nc = tc.nc
+    with ExitStack() as ctx:
+        keep = ctx.enter_context(tc.tile_pool(name="keep", bufs=1))
+        weight_rows = ctx.enter_context(tc.tile_pool(name="weight_rows", bufs=2 * HALVES))
+        query_rows = ctx.enter_context(tc.tile_pool(name="query_rows", bufs=QUERY_BUFFERS))
+        regroup = ctx.enter_context(tc.tile_pool(name="regroup", bufs=3))
+        query_mx = ctx.enter_context(tc.tile_pool(name="query_mx", bufs=AHEAD + 2))
+        gates = ctx.enter_context(tc.tile_pool(name="gates", bufs=3))
+        answers = ctx.enter_context(tc.tile_pool(name="answers", bufs=3))
+        stats = ctx.enter_context(tc.tile_pool(name="stats", bufs=3))
+        turn_banks = ctx.enter_context(tc.psum_pool(name="turn_banks", bufs=4))
+        sum_banks = ctx.enter_context(tc.psum_pool(name="sum_banks", bufs=4))
+
+        identity = keep.tile([P, P], F32)
+        make_identity(nc, identity[:])
+
+        def load_rows(pool, rows, label):
+            raw = pool.tile([P, TILES, FEATURES], BF16, name=label)
+            nc.sync.dma_start(out=raw[:], in_=rows.rearrange("(n p) k -> p n k", p=P))
+            return raw
+
+        def load_queries(c):
+            raw = query_rows.tile([P, TILES, FEATURES], BF16, name="query_raw")
+            nc.sync.dma_start(out=raw[:], in_=queries[:, c * TILES : (c + 1) * TILES, :])
+            return raw
+
+        def new_operand(pool, label):
+            codes = pool.tile([P, CHUNK_WORDS], U32, name=label + "_codes", align_bytes=64)
+            scales = pool.tile([P, CHUNK_WORDS], U8, name=label + "_scales", align_bytes=64)
+            return codes, scales
+
+        def quantise_rows(raw, operand, order):
+            codes, scales = operand
+            grouped = regroup.tile([P, CHUNK_WORDS * PACK], BF16, tag="grouped", align_bytes=64)
+            pairs = grouped[:].bitcast(F32).rearrange(
+                "p (" + order + " u) -> p n g r u", n=TILES, g=PASSES, u=2
+            )
+            row_words = raw[:].bitcast(F32)
+            for n in range(TILES):
+                turned = turn_banks.tile([P, PASSES * 2, P], F32, tag="turned")
+                for j in range(PASSES * 2):
+                    nc.tensor.transpose(turned[:, j, :], row_words[:, n, j * P : (j + 1) * P], identity[:])
+                nc.scalar.copy(out=pairs[:, n], in_=turned[:].rearrange("p (g u) r -> p g r u", u=2))
+            nc.vector.quantize_mx(out=codes[:].bitcast(FP8X4), scales=scales[:], in_=grouped[:])
+
+        memory_raw = load_rows(keep, memory_items, "memory_raw")
+        pooled_raw = load_rows(keep, wq, "pooled_raw")
+        u_raw = []
+        w_raw = []
+        for h in range(HALVES):
+            half_rows = slice(h * CHUNK_ROWS, (h + 1) * CHUNK_ROWS)
+            u_half = load_rows(weight_rows, U_w[half_rows, :], "weight_raw")
+            w_half = load_rows(weight_rows, W_w[half_rows, :], "weight_raw")
+            u_raw.append(u_half)
+            w_raw.append(w_half)
+        query_raw = {}
+        for c in range(QUERY_BUFFERS):
+            query_raw[c] = load_queries(c)
+
+        memory_mx = new_operand(keep, "memory")
+        pooled_mx = new_operand(keep, "pooled")
+        quantise_rows(memory_raw, memory_mx, "n g r")
+        quantise_rows(pooled_raw, pooled_mx, "n g r")
+        step = keep.tile([P, TILES, FEATURES], F32)
+        for n in range(TILES):
+            nc.vector.tensor_sub(out=step[:, n, :], in0=pooled_raw[:, n, :], in1=memory_raw[:, n, :])
+
+        new_slots = keep.tile([P, TILES, FEATURES], F32)
+        new_mx = new_operand(keep, "new_slots")
+        out_0_tiles = out_0.rearrange("(n p) k -> p n k", p=P)
+
+        def gate_products(h, u_mx, w_mx):
+            sums = []
+            for n in range(TILES):
+                total = sum_banks.tile([P, CHUNK_ROWS], F32, tag="total")
+                sums.append(total)
+            for first, (slot_mx, weight_mx) in ((True, (memory_mx, u_mx)), (False, (pooled_mx, w_mx))):
+                for n in range(TILES):
+                    for g in range(PASSES):
+                        nc.tensor.matmul_mx(
+                            out=sums[n][:],
+                            lhsT=slot_mx[0][:, stationary_cols(n, g)].bitcast(FP8X4),
+                            lhsT_scale=slot_mx[1][:, stationary_cols(n, g)],
+                            rhs=weight_mx[0][:, moving_cols(g)].bitcast(FP8X4),
+                            rhs_scale=weight_mx[1][:, moving_cols(g)],
+                            start=(first and g == 0),
+                            stop=(not first and g == PASSES - 1),
+                        )
+            return sums
+
+        def blend(h, sums):
+            cols = slice(h * CHUNK_ROWS, (h + 1) * CHUNK_ROWS)
+            for n in range(TILES):
+                gate = gates.tile([P, CHUNK_ROWS], F32)
+                nc.scalar.activation(out=gate[:], in_=sums[n][:], func=ACT.Sigmoid)
+                nc.vector.tensor_mul(out=gate[:], in0=gate[:], in1=step[:, n, cols])
+                nc.vector.tensor_add(out=new_slots[:, n, cols], in0=gate[:], in1=memory_raw[:, n, cols])
+            nc.sync.dma_start(out=out_0_tiles[:, :, cols], in_=new_slots[:, :, cols])
+
+        def quantise_new_slots(g):
+            grouped = regroup.tile([P, SLOTS, PACK], BF16, tag="grouped", align_bytes=64)
+            for n in range(TILES):
+                by_code = new_slots[:, n, g * K_PASS : (g + 1) * K_PASS].rearrange(
+                    "p (u q e) -> p u e q", u=2, e=2
+                )
+                turned = turn_banks.tile([P, PACK, P], F32, tag="turned")
+                for u in range(2):
+                    for e in range(2):
+                        nc.tensor.transpose(turned[:, 2 * u + e, :], by_code[:, u, e, :], identity[:])
+                nc.scalar.copy(
+                    out=grouped[:, n * P : (n + 1) * P, :], in_=turned[:].rearrange("p t r -> p r t")
+                )
+            nc.vector.quantize_mx(
+                out=new_mx[0][:, moving_cols(g)].bitcast(FP8X4),
+                scales=new_mx[1][:, moving_cols(g)],
+                in_=grouped[:].rearrange("p m t -> p (m t)"),
+            )
+
+        queries_mx = {}
+
+        def quantise_queries(c):
+            queries_mx[c] = new_operand(query_mx, "query")
+            quantise_rows(query_raw[c], queries_mx[c], "n g r")
+            if c + QUERY_BUFFERS < QUERY_CHUNKS:
+                query_raw[c + QUERY_BUFFERS] = load_queries(c + QUERY_BUFFERS)
+
+        def attend(c):
+            codes, scales = queries_mx[c]
+            answer = answers.tile([P, TILES, SLOTS], F32)
+            row_max = stats.tile([P, TILES], F32)
+            shift = stats.tile([P, TILES], F32)
+            row_sum = stats.tile([P, TILES], F32)
+            inverse = stats.tile([P, TILES], F32)
+            sums = []
+            for n in range(TILES):
+                total = sum_banks.tile([P, SLOTS], F32, tag="total")
+                for g in range(PASSES):
+                    nc.tensor.matmul_mx(
+                        out=total[:],
+                        lhsT=codes[:, stationary_cols(n, g)].bitcast(FP8X4),
+                        lhsT_scale=scales[:, stationary_cols(n, g)],
+                        rhs=new_mx[0][:, moving_cols(g)].bitcast(FP8X4),
+                        rhs_scale=new_mx[1][:, moving_cols(g)],
+                        start=(g == 0),
+                        stop=(g == PASSES - 1),
+                    )
+                nc.vector.reduce_max(out=row_max[:, n : n + 1], in_=total[:], axis=AXIS.X)
+                sums.append(total)
+            nc.vector.tensor_scalar_mul(out=shift[:], in0=row_max[:], scalar1=-1.0 / TEMPERATURE)
+            for n in range(TILES):
+                nc.scalar.activation(
+                    out=answer[:, n, :],
+                    in_=sums[n][:],
+                    func=ACT.Exp,
+                    bias=shift[:, n : n + 1],
+                    scale=1.0 / TEMPERATURE,
+                    accum_out=row_sum[:, n : n + 1],
+                )
+            nc.vector.reciprocal(out=inverse[:], in_=row_sum[:])
+            for n in range(TILES):
+                nc.vector.tensor_scalar_mul(
+                    out=answer[:, n, :], in0=answer[:, n, :], scalar1=inverse[:, n : n + 1]
+                )
+            nc.sync.dma_start(out=out_1[:, c * TILES : (c + 1) * TILES, :], in_=answer[:])
+
+        for h in range(HALVES):
+            u_mx = new_operand(keep, "u%d" % h)
+            w_mx = new_operand(keep, "w%d" % h)
+            quantise_rows(u_raw[h], u_mx, "g n r")
+            quantise_rows(w_raw[h], w_mx, "g n r")
+            sums = gate_products(h, u_mx, w_mx)
+            blend(h, sums)
+            quantise_new_slots(h)
+
+        for c in range(AHEAD):
+            quantise_queries(c)
+        for c in range(QUERY_CHUNKS):
+            if c + AHEAD < QUERY_CHUNKS:
+                quantise_queries(c + AHEAD)
+            attend(c)

@@ -9,7 +9,7 @@ U32 = mybir.dt.uint32
 U8 = mybir.dt.uint8
 FP8X4 = mybir.dt.float8_e4m3fn_x4
 ACT = mybir.ActivationFunctionType
-AXIS = mybir.AxisListType
+ALU = mybir.AluOpType
 
 P = 128
 FEATURES = 1024
@@ -25,7 +25,7 @@ CHUNK_WORDS = CHUNK_ROWS * PASSES
 HALVES = FEATURES // CHUNK_ROWS
 QUERY_CHUNKS = BATCH // TILES
 QUERY_BUFFERS = 4
-AHEAD = 2
+STORE_TILES = 2
 
 FLOPS = 2 * (2 * SLOTS * FEATURES * FEATURES) + 2 * (P * BATCH) * SLOTS * FEATURES
 
@@ -45,12 +45,13 @@ def tile_gatedmemorymodule_pb_t_kernel(tc, queries, memory_items, wq, U_w, W_w, 
         weight_rows = ctx.enter_context(tc.tile_pool(name="weight_rows", bufs=2 * HALVES))
         query_rows = ctx.enter_context(tc.tile_pool(name="query_rows", bufs=QUERY_BUFFERS))
         regroup = ctx.enter_context(tc.tile_pool(name="regroup", bufs=3))
-        query_mx = ctx.enter_context(tc.tile_pool(name="query_mx", bufs=AHEAD + 2))
+        query_mx = ctx.enter_context(tc.tile_pool(name="query_mx", bufs=4))
         gates = ctx.enter_context(tc.tile_pool(name="gates", bufs=3))
         answers = ctx.enter_context(tc.tile_pool(name="answers", bufs=3))
         stats = ctx.enter_context(tc.tile_pool(name="stats", bufs=3))
-        turn_banks = ctx.enter_context(tc.psum_pool(name="turn_banks", bufs=4))
-        sum_banks = ctx.enter_context(tc.psum_pool(name="sum_banks", bufs=4))
+        turn_banks = ctx.enter_context(tc.psum_pool(name="turn_banks", bufs=TILES))
+        sum_banks = ctx.enter_context(tc.psum_pool(name="sum_banks", bufs=TILES))
+        ctx.enter_context(tc.manual_schedule())
 
         identity = keep.tile([P, P], F32)
         make_identity(nc, identity[:])
@@ -70,152 +71,269 @@ def tile_gatedmemorymodule_pb_t_kernel(tc, queries, memory_items, wq, U_w, W_w, 
             scales = pool.tile([P, CHUNK_WORDS], U8, name=label + "_scales", align_bytes=64)
             return codes, scales
 
-        def quantise_rows(raw, operand, order):
-            codes, scales = operand
-            grouped = regroup.tile([P, CHUNK_WORDS * PACK], BF16, tag="grouped", align_bytes=64)
-            pairs = grouped[:].bitcast(F32).rearrange(
-                "p (" + order + " u) -> p n g r u", n=TILES, g=PASSES, u=2
-            )
-            row_words = raw[:].bitcast(F32)
+        def input_chunk(raw, operand, order):
+            words = raw[:].bitcast(F32)
+            return {
+                "blocks": [[words[:, n, j * P : (j + 1) * P] for j in range(PACK)] for n in range(TILES)],
+                "order": order,
+                "codes": operand[0][:],
+                "scales": operand[1][:],
+                "banks": [],
+            }
+
+        def slots_chunk(g):
+            blocks = []
             for n in range(TILES):
-                turned = turn_banks.tile([P, PASSES * 2, P], F32, tag="turned")
-                for j in range(PASSES * 2):
-                    nc.tensor.transpose(turned[:, j, :], row_words[:, n, j * P : (j + 1) * P], identity[:])
-                nc.scalar.copy(out=pairs[:, n], in_=turned[:].rearrange("p (g u) r -> p g r u", u=2))
-            nc.vector.quantize_mx(out=codes[:].bitcast(FP8X4), scales=scales[:], in_=grouped[:])
+                by_code = new_slots[:, n, g * K_PASS : (g + 1) * K_PASS].rearrange(
+                    "p (u q e) -> p u e q", u=2, e=2
+                )
+                blocks.append([by_code[:, t // 2, t % 2, :] for t in range(PACK)])
+            return {
+                "blocks": blocks,
+                "order": None,
+                "codes": new_mx[0][:, moving_cols(g)],
+                "scales": new_mx[1][:, moving_cols(g)],
+                "banks": [],
+            }
+
+        def turn(chunk, n):
+            turned = turn_banks.tile([P, PACK, P], F32, tag="turned")
+            for j in range(PACK):
+                nc.tensor.transpose(turned[:, j, :], chunk["blocks"][n][j], identity[:])
+            chunk["banks"].append(turned)
+
+        def make_room(chunk):
+            if chunk["order"] is None:
+                grouped = regroup.tile([P, SLOTS * PACK], BF16, tag="grouped", align_bytes=64)
+                chunk["targets"] = grouped[:].rearrange("p (n g r t) -> p n g r t", n=TILES, g=1, t=PACK)
+                chunk["side_by_side"] = PACK
+            else:
+                grouped = regroup.tile([P, CHUNK_WORDS * PACK], BF16, tag="grouped", align_bytes=64)
+                chunk["targets"] = grouped[:].bitcast(F32).rearrange(
+                    "p (" + chunk["order"] + " u) -> p n g r u", n=TILES, g=PASSES, u=2
+                )
+                chunk["side_by_side"] = 2
+            chunk["grouped"] = grouped
+
+        def copy_out(chunk, n, engine_copy):
+            engine_copy(
+                out=chunk["targets"][:, n],
+                in_=chunk["banks"][n][:].rearrange("p (g u) r -> p g r u", u=chunk["side_by_side"]),
+            )
+
+        def roll(leaving, entering, vector_helps):
+            if leaving is not None:
+                make_room(leaving)
+            for n in range(TILES):
+                if leaving is not None:
+                    if vector_helps and n == TILES - 1:
+                        copy_out(leaving, n, nc.vector.tensor_copy)
+                    else:
+                        copy_out(leaving, n, nc.scalar.copy)
+                if entering is not None:
+                    turn(entering, n)
+
+        def quantise(chunk):
+            nc.vector.quantize_mx(
+                out=chunk["codes"].bitcast(FP8X4), scales=chunk["scales"], in_=chunk["grouped"][:]
+            )
+
+        def products(total, n, slot_mx, weight_mx, first):
+            for g in range(PASSES):
+                nc.tensor.matmul_mx(
+                    out=total[:],
+                    lhsT=slot_mx[0][:, stationary_cols(n, g)].bitcast(FP8X4),
+                    lhsT_scale=slot_mx[1][:, stationary_cols(n, g)],
+                    rhs=weight_mx[0][:, moving_cols(g)].bitcast(FP8X4),
+                    rhs_scale=weight_mx[1][:, moving_cols(g)],
+                    start=(first and g == 0),
+                    stop=(not first and g == PASSES - 1),
+                )
+
+        def blend(h, n, total):
+            cols = slice(h * CHUNK_ROWS, (h + 1) * CHUNK_ROWS)
+            lift = gates.tile([P, CHUNK_ROWS], F32)
+            nc.scalar.activation(out=lift[:], in_=total[:], func=ACT.Tanh, scale=0.5)
+            nc.vector.scalar_tensor_tensor(
+                out=lift[:], in0=lift[:], scalar=1.0, in1=step[:, n, cols], op0=ALU.add, op1=ALU.mult
+            )
+            nc.vector.scalar_tensor_tensor(
+                out=new_slots[:, n, cols], in0=lift[:], scalar=0.5, in1=memory_raw[:, n, cols],
+                op0=ALU.mult, op1=ALU.add,
+            )
+
+        def store_slots(h):
+            cols = slice(h * CHUNK_ROWS, (h + 1) * CHUNK_ROWS)
+            nc.sync.dma_start(
+                out=out_0.rearrange("(n p) k -> p n k", p=P)[:, :, cols], in_=new_slots[:, :, cols]
+            )
+
+        query_raw = {}
+        query = {}
+
+        def query_chunk(c):
+            if c >= QUERY_CHUNKS:
+                return None
+            if c not in query:
+                query[c] = input_chunk(query_raw[c], new_operand(query_mx, "query"), "n g r")
+            return query[c]
+
+        def refill(c):
+            if c + QUERY_BUFFERS < QUERY_CHUNKS:
+                query_raw[c + QUERY_BUFFERS] = load_queries(c + QUERY_BUFFERS)
+
+        def begin_answer(c):
+            answer = answers.tile([P, TILES, SLOTS], F32)
+            shift = stats.tile([P, TILES], F32)
+            row_sum = stats.tile([P, TILES], F32)
+            inverse = stats.tile([P, TILES], F32)
+            query[c]["answer"] = answer
+            query[c]["shift"] = shift
+            query[c]["row_sum"] = row_sum
+            query[c]["inverse"] = inverse
+            query[c]["sums"] = []
+
+        def multiply(c, n):
+            total = sum_banks.tile([P, SLOTS], F32, tag="total")
+            for g in range(PASSES):
+                nc.tensor.matmul_mx(
+                    out=total[:],
+                    lhsT=query[c]["codes"][:, stationary_cols(n, g)].bitcast(FP8X4),
+                    lhsT_scale=query[c]["scales"][:, stationary_cols(n, g)],
+                    rhs=new_mx[0][:, moving_cols(g)].bitcast(FP8X4),
+                    rhs_scale=new_mx[1][:, moving_cols(g)],
+                    start=(g == 0),
+                    stop=(g == PASSES - 1),
+                )
+            query[c]["sums"].append(total)
+
+        def leave_bank(c, n):
+            nc.vector.tensor_scalar(
+                out=query[c]["answer"][:, n, :],
+                in0=query[c]["sums"][n][:],
+                scalar1=-1.0 / TEMPERATURE,
+                scalar2=None,
+                op0=ALU.mult,
+                op1=ALU.min,
+                accum_out=query[c]["shift"][:, n : n + 1],
+            )
+
+        def exponential(c, n):
+            nc.scalar.activation(
+                out=query[c]["answer"][:, n, :],
+                in_=query[c]["answer"][:, n, :],
+                func=ACT.Exp,
+                bias=query[c]["shift"][:, n : n + 1],
+                scale=-1.0,
+                accum_out=query[c]["row_sum"][:, n : n + 1],
+            )
+
+        def normalise(c):
+            nc.vector.reciprocal(out=query[c]["inverse"][:], in_=query[c]["row_sum"][:])
+            for n in range(TILES):
+                row = query[c]["answer"][:, n, :]
+                factor = query[c]["inverse"][:, n : n + 1]
+                if c == QUERY_CHUNKS - 1:
+                    nc.vector.tensor_scalar_mul(out=row, in0=row, scalar1=factor)
+                else:
+                    nc.gpsimd.tensor_scalar(
+                        out=row, in0=row, scalar1=factor, scalar2=0.0, op0=ALU.mult, op1=ALU.add
+                    )
+                if (n + 1) % STORE_TILES == 0:
+                    done = slice(n + 1 - STORE_TILES, n + 1)
+                    entries = slice(c * TILES + n + 1 - STORE_TILES, c * TILES + n + 1)
+                    nc.sync.dma_start(out=out_1[:, entries, :], in_=query[c]["answer"][:, done, :])
 
         memory_raw = load_rows(keep, memory_items, "memory_raw")
+        u_raw = [load_rows(weight_rows, U_w[0:CHUNK_ROWS, :], "weight_raw")]
         pooled_raw = load_rows(keep, wq, "pooled_raw")
-        u_raw = []
-        w_raw = []
-        for h in range(HALVES):
-            half_rows = slice(h * CHUNK_ROWS, (h + 1) * CHUNK_ROWS)
-            u_half = load_rows(weight_rows, U_w[half_rows, :], "weight_raw")
-            w_half = load_rows(weight_rows, W_w[half_rows, :], "weight_raw")
-            u_raw.append(u_half)
-            w_raw.append(w_half)
-        query_raw = {}
+        w_raw = [load_rows(weight_rows, W_w[0:CHUNK_ROWS, :], "weight_raw")]
+        u_raw.append(load_rows(weight_rows, U_w[CHUNK_ROWS:FEATURES, :], "weight_raw"))
+        w_raw.append(load_rows(weight_rows, W_w[CHUNK_ROWS:FEATURES, :], "weight_raw"))
         for c in range(QUERY_BUFFERS):
             query_raw[c] = load_queries(c)
 
         memory_mx = new_operand(keep, "memory")
         pooled_mx = new_operand(keep, "pooled")
-        quantise_rows(memory_raw, memory_mx, "n g r")
-        quantise_rows(pooled_raw, pooled_mx, "n g r")
+        u_mx = [new_operand(keep, "u%d" % h) for h in range(HALVES)]
+        w_mx = [new_operand(keep, "w%d" % h) for h in range(HALVES)]
+        new_mx = new_operand(keep, "new_slots")
         step = keep.tile([P, TILES, FEATURES], F32)
-        for n in range(TILES):
+        new_slots = keep.tile([P, TILES, FEATURES], F32)
+
+        memory_chunk = input_chunk(memory_raw, memory_mx, "n g r")
+        pooled_chunk = input_chunk(pooled_raw, pooled_mx, "n g r")
+        u_chunk = [input_chunk(u_raw[h], u_mx[h], "g n r") for h in range(HALVES)]
+        w_chunk = [input_chunk(w_raw[h], w_mx[h], "g n r") for h in range(HALVES)]
+        new_chunk = [slots_chunk(g) for g in range(PASSES)]
+
+        def difference(n):
             nc.vector.tensor_sub(out=step[:, n, :], in0=pooled_raw[:, n, :], in1=memory_raw[:, n, :])
 
-        new_slots = keep.tile([P, TILES, FEATURES], F32)
-        new_mx = new_operand(keep, "new_slots")
-        out_0_tiles = out_0.rearrange("(n p) k -> p n k", p=P)
+        roll(None, memory_chunk, False)
+        roll(memory_chunk, u_chunk[0], False)
+        quantise(memory_chunk)
+        roll(u_chunk[0], pooled_chunk, False)
+        quantise(u_chunk[0])
+        roll(pooled_chunk, w_chunk[0], False)
+        quantise(pooled_chunk)
+        sums = []
+        for n in range(TILES):
+            total = sum_banks.tile([P, CHUNK_ROWS], F32, tag="total")
+            sums.append(total)
+            products(total, n, memory_mx, u_mx[0], True)
+        difference(0)
+        difference(1)
+        roll(w_chunk[0], u_chunk[1], False)
+        quantise(w_chunk[0])
+        difference(2)
+        difference(3)
+        roll(u_chunk[1], w_chunk[1], False)
+        for n in range(TILES):
+            products(sums[n], n, pooled_mx, w_mx[0], False)
+        quantise(u_chunk[1])
+        roll(w_chunk[1], query_chunk(0), False)
+        refill(0)
+        quantise(w_chunk[1])
+        next_sums = []
+        for n in range(TILES):
+            blend(0, n, sums[n])
+            total = sum_banks.tile([P, CHUNK_ROWS], F32, tag="total")
+            next_sums.append(total)
+            products(total, n, memory_mx, u_mx[1], True)
+        store_slots(0)
+        for n in range(TILES):
+            products(next_sums[n], n, pooled_mx, w_mx[1], False)
+        roll(query_chunk(0), new_chunk[0], False)
+        quantise(query_chunk(0))
+        for n in range(TILES):
+            blend(1, n, next_sums[n])
+        store_slots(1)
+        roll(new_chunk[0], new_chunk[1], False)
+        quantise(new_chunk[0])
+        roll(new_chunk[1], query_chunk(1), False)
+        refill(1)
+        quantise(new_chunk[1])
 
-        def gate_products(h, u_mx, w_mx):
-            sums = []
-            for n in range(TILES):
-                total = sum_banks.tile([P, CHUNK_ROWS], F32, tag="total")
-                sums.append(total)
-            for first, (slot_mx, weight_mx) in ((True, (memory_mx, u_mx)), (False, (pooled_mx, w_mx))):
-                for n in range(TILES):
-                    for g in range(PASSES):
-                        nc.tensor.matmul_mx(
-                            out=sums[n][:],
-                            lhsT=slot_mx[0][:, stationary_cols(n, g)].bitcast(FP8X4),
-                            lhsT_scale=slot_mx[1][:, stationary_cols(n, g)],
-                            rhs=weight_mx[0][:, moving_cols(g)].bitcast(FP8X4),
-                            rhs_scale=weight_mx[1][:, moving_cols(g)],
-                            start=(first and g == 0),
-                            stop=(not first and g == PASSES - 1),
-                        )
-            return sums
-
-        def blend(h, sums):
-            cols = slice(h * CHUNK_ROWS, (h + 1) * CHUNK_ROWS)
-            for n in range(TILES):
-                gate = gates.tile([P, CHUNK_ROWS], F32)
-                nc.scalar.activation(out=gate[:], in_=sums[n][:], func=ACT.Sigmoid)
-                nc.vector.tensor_mul(out=gate[:], in0=gate[:], in1=step[:, n, cols])
-                nc.vector.tensor_add(out=new_slots[:, n, cols], in0=gate[:], in1=memory_raw[:, n, cols])
-            nc.sync.dma_start(out=out_0_tiles[:, :, cols], in_=new_slots[:, :, cols])
-
-        def quantise_new_slots(g):
-            grouped = regroup.tile([P, SLOTS, PACK], BF16, tag="grouped", align_bytes=64)
-            for n in range(TILES):
-                by_code = new_slots[:, n, g * K_PASS : (g + 1) * K_PASS].rearrange(
-                    "p (u q e) -> p u e q", u=2, e=2
-                )
-                turned = turn_banks.tile([P, PACK, P], F32, tag="turned")
-                for u in range(2):
-                    for e in range(2):
-                        nc.tensor.transpose(turned[:, 2 * u + e, :], by_code[:, u, e, :], identity[:])
-                nc.scalar.copy(
-                    out=grouped[:, n * P : (n + 1) * P, :], in_=turned[:].rearrange("p t r -> p r t")
-                )
-            nc.vector.quantize_mx(
-                out=new_mx[0][:, moving_cols(g)].bitcast(FP8X4),
-                scales=new_mx[1][:, moving_cols(g)],
-                in_=grouped[:].rearrange("p m t -> p (m t)"),
-            )
-
-        queries_mx = {}
-
-        def quantise_queries(c):
-            queries_mx[c] = new_operand(query_mx, "query")
-            quantise_rows(query_raw[c], queries_mx[c], "n g r")
-            if c + QUERY_BUFFERS < QUERY_CHUNKS:
-                query_raw[c + QUERY_BUFFERS] = load_queries(c + QUERY_BUFFERS)
-
-        def attend(c):
-            codes, scales = queries_mx[c]
-            answer = answers.tile([P, TILES, SLOTS], F32)
-            row_max = stats.tile([P, TILES], F32)
-            shift = stats.tile([P, TILES], F32)
-            row_sum = stats.tile([P, TILES], F32)
-            inverse = stats.tile([P, TILES], F32)
-            sums = []
-            for n in range(TILES):
-                total = sum_banks.tile([P, SLOTS], F32, tag="total")
-                for g in range(PASSES):
-                    nc.tensor.matmul_mx(
-                        out=total[:],
-                        lhsT=codes[:, stationary_cols(n, g)].bitcast(FP8X4),
-                        lhsT_scale=scales[:, stationary_cols(n, g)],
-                        rhs=new_mx[0][:, moving_cols(g)].bitcast(FP8X4),
-                        rhs_scale=new_mx[1][:, moving_cols(g)],
-                        start=(g == 0),
-                        stop=(g == PASSES - 1),
-                    )
-                nc.vector.reduce_max(out=row_max[:, n : n + 1], in_=total[:], axis=AXIS.X)
-                sums.append(total)
-            nc.vector.tensor_scalar_mul(out=shift[:], in0=row_max[:], scalar1=-1.0 / TEMPERATURE)
-            for n in range(TILES):
-                nc.scalar.activation(
-                    out=answer[:, n, :],
-                    in_=sums[n][:],
-                    func=ACT.Exp,
-                    bias=shift[:, n : n + 1],
-                    scale=1.0 / TEMPERATURE,
-                    accum_out=row_sum[:, n : n + 1],
-                )
-            nc.vector.reciprocal(out=inverse[:], in_=row_sum[:])
-            for n in range(TILES):
-                nc.vector.tensor_scalar_mul(
-                    out=answer[:, n, :], in0=answer[:, n, :], scalar1=inverse[:, n : n + 1]
-                )
-            nc.sync.dma_start(out=out_1[:, c * TILES : (c + 1) * TILES, :], in_=answer[:])
-
-        for h in range(HALVES):
-            u_mx = new_operand(keep, "u%d" % h)
-            w_mx = new_operand(keep, "w%d" % h)
-            quantise_rows(u_raw[h], u_mx, "g n r")
-            quantise_rows(w_raw[h], w_mx, "g n r")
-            sums = gate_products(h, u_mx, w_mx)
-            blend(h, sums)
-            quantise_new_slots(h)
-
-        for c in range(AHEAD):
-            quantise_queries(c)
+        begin_answer(0)
+        for n in range(TILES):
+            multiply(0, n)
+        roll(query_chunk(1), query_chunk(2), False)
+        refill(2)
+        quantise(query_chunk(1))
+        roll(query_chunk(2), query_chunk(3), False)
+        refill(3)
         for c in range(QUERY_CHUNKS):
-            if c + AHEAD < QUERY_CHUNKS:
-                quantise_queries(c + AHEAD)
-            attend(c)
+            if c + 1 < QUERY_CHUNKS:
+                begin_answer(c + 1)
+            for n in range(TILES):
+                leave_bank(c, n)
+                if c + 1 < QUERY_CHUNKS:
+                    multiply(c + 1, n)
+                exponential(c, n)
+            if c + 3 < QUERY_CHUNKS:
+                roll(query_chunk(c + 3), query_chunk(c + 4), True)
+                refill(c + 4)
+            if c + 2 < QUERY_CHUNKS:
+                quantise(query_chunk(c + 2))
+            normalise(c)

@@ -38,6 +38,14 @@ def moving_cols(g):
     return slice(g * CHUNK_ROWS, (g + 1) * CHUNK_ROWS)
 
 
+def in_tile_order(bank):
+    return bank.rearrange("p (n r) -> p r n", n=TILES)
+
+
+def in_row_order(row):
+    return row.rearrange("p (r n) -> p r n", n=TILES)
+
+
 def tile_gatedmemorymodule_pb_t_kernel(tc, queries, memory_items, wq, U_w, W_w, out_0, out_1):
     nc = tc.nc
     with ExitStack() as ctx:
@@ -58,7 +66,7 @@ def tile_gatedmemorymodule_pb_t_kernel(tc, queries, memory_items, wq, U_w, W_w, 
 
         def load_rows(pool, rows, label):
             raw = pool.tile([P, TILES, FEATURES], BF16, name=label)
-            nc.sync.dma_start(out=raw[:], in_=rows.rearrange("(n p) k -> p n k", p=P))
+            nc.sync.dma_start(out=raw[:], in_=rows.rearrange("(p n) k -> p n k", n=TILES))
             return raw
 
         def load_queries(c):
@@ -153,7 +161,7 @@ def tile_gatedmemorymodule_pb_t_kernel(tc, queries, memory_items, wq, U_w, W_w, 
         def blend(h, n, total):
             cols = slice(h * CHUNK_ROWS, (h + 1) * CHUNK_ROWS)
             lift = gates.tile([P, CHUNK_ROWS], F32)
-            nc.scalar.activation(out=lift[:], in_=total[:], func=ACT.Tanh, scale=0.5)
+            nc.scalar.activation(out=in_row_order(lift[:]), in_=in_tile_order(total[:]), func=ACT.Tanh, scale=0.5)
             nc.vector.scalar_tensor_tensor(
                 out=lift[:], in0=lift[:], scalar=1.0, in1=step[:, n, cols], op0=ALU.add, op1=ALU.mult
             )
@@ -165,7 +173,7 @@ def tile_gatedmemorymodule_pb_t_kernel(tc, queries, memory_items, wq, U_w, W_w, 
         def store_slots(h):
             cols = slice(h * CHUNK_ROWS, (h + 1) * CHUNK_ROWS)
             nc.sync.dma_start(
-                out=out_0.rearrange("(n p) k -> p n k", p=P)[:, :, cols], in_=new_slots[:, :, cols]
+                out=out_0.rearrange("(p n) k -> p n k", n=TILES)[:, :, cols], in_=new_slots[:, :, cols]
             )
 
         query_raw = {}
@@ -209,8 +217,8 @@ def tile_gatedmemorymodule_pb_t_kernel(tc, queries, memory_items, wq, U_w, W_w, 
 
         def leave_bank(c, n):
             nc.vector.tensor_scalar(
-                out=query[c]["answer"][:, n, :],
-                in0=query[c]["sums"][n][:],
+                out=in_row_order(query[c]["answer"][:, n, :]),
+                in0=in_tile_order(query[c]["sums"][n][:]),
                 scalar1=-1.0 / TEMPERATURE,
                 scalar2=None,
                 op0=ALU.mult,
@@ -245,8 +253,8 @@ def tile_gatedmemorymodule_pb_t_kernel(tc, queries, memory_items, wq, U_w, W_w, 
                     nc.sync.dma_start(out=out_1[:, entries, :], in_=query[c]["answer"][:, done, :])
 
         memory_raw = load_rows(keep, memory_items, "memory_raw")
-        u_raw = [load_rows(weight_rows, U_w[0:CHUNK_ROWS, :], "weight_raw")]
         pooled_raw = load_rows(keep, wq, "pooled_raw")
+        u_raw = [load_rows(weight_rows, U_w[0:CHUNK_ROWS, :], "weight_raw")]
         w_raw = [load_rows(weight_rows, W_w[0:CHUNK_ROWS, :], "weight_raw")]
         u_raw.append(load_rows(weight_rows, U_w[CHUNK_ROWS:FEATURES, :], "weight_raw"))
         w_raw.append(load_rows(weight_rows, W_w[CHUNK_ROWS:FEATURES, :], "weight_raw"))
@@ -271,24 +279,24 @@ def tile_gatedmemorymodule_pb_t_kernel(tc, queries, memory_items, wq, U_w, W_w, 
             nc.vector.tensor_sub(out=step[:, n, :], in0=pooled_raw[:, n, :], in1=memory_raw[:, n, :])
 
         roll(None, memory_chunk, False)
-        roll(memory_chunk, u_chunk[0], False)
+        roll(memory_chunk, pooled_chunk, False)
         quantise(memory_chunk)
-        roll(u_chunk[0], pooled_chunk, False)
-        quantise(u_chunk[0])
-        roll(pooled_chunk, w_chunk[0], False)
+        difference(0)
+        roll(pooled_chunk, u_chunk[0], False)
         quantise(pooled_chunk)
+        difference(1)
+        roll(u_chunk[0], w_chunk[0], False)
+        quantise(u_chunk[0])
+        difference(2)
+        roll(w_chunk[0], u_chunk[1], False)
+        quantise(w_chunk[0])
+        difference(3)
+        roll(u_chunk[1], w_chunk[1], False)
         sums = []
         for n in range(TILES):
             total = sum_banks.tile([P, CHUNK_ROWS], F32, tag="total")
             sums.append(total)
             products(total, n, memory_mx, u_mx[0], True)
-        difference(0)
-        difference(1)
-        roll(w_chunk[0], u_chunk[1], False)
-        quantise(w_chunk[0])
-        difference(2)
-        difference(3)
-        roll(u_chunk[1], w_chunk[1], False)
         for n in range(TILES):
             products(sums[n], n, pooled_mx, w_mx[0], False)
         quantise(u_chunk[1])

@@ -201,19 +201,23 @@ def tile_gatedmemorymodule_pb_t_kernel(tc, queries, memory_items, wq, U_w, W_w, 
             query[c]["inverse"] = inverse
             query[c]["sums"] = []
 
+        def logit_pass(c, n, g):
+            if g == 0:
+                total = sum_banks.tile([P, SLOTS], F32, tag="total")
+                query[c]["sums"].append(total)
+            nc.tensor.matmul_mx(
+                out=query[c]["sums"][n][:],
+                lhsT=query[c]["codes"][:, stationary_cols(n, g)].bitcast(FP8X4),
+                lhsT_scale=query[c]["scales"][:, stationary_cols(n, g)],
+                rhs=new_mx[0][:, moving_cols(g)].bitcast(FP8X4),
+                rhs_scale=new_mx[1][:, moving_cols(g)],
+                start=(g == 0),
+                stop=(g == PASSES - 1),
+            )
+
         def multiply(c, n):
-            total = sum_banks.tile([P, SLOTS], F32, tag="total")
             for g in range(PASSES):
-                nc.tensor.matmul_mx(
-                    out=total[:],
-                    lhsT=query[c]["codes"][:, stationary_cols(n, g)].bitcast(FP8X4),
-                    lhsT_scale=query[c]["scales"][:, stationary_cols(n, g)],
-                    rhs=new_mx[0][:, moving_cols(g)].bitcast(FP8X4),
-                    rhs_scale=new_mx[1][:, moving_cols(g)],
-                    start=(g == 0),
-                    stop=(g == PASSES - 1),
-                )
-            query[c]["sums"].append(total)
+                logit_pass(c, n, g)
 
         def leave_bank(c, n):
             nc.vector.tensor_scalar(
@@ -253,8 +257,8 @@ def tile_gatedmemorymodule_pb_t_kernel(tc, queries, memory_items, wq, U_w, W_w, 
                     nc.sync.dma_start(out=out_1[:, entries, :], in_=query[c]["answer"][:, done, :])
 
         memory_raw = load_rows(keep, memory_items, "memory_raw")
-        pooled_raw = load_rows(keep, wq, "pooled_raw")
         u_raw = [load_rows(weight_rows, U_w[0:CHUNK_ROWS, :], "weight_raw")]
+        pooled_raw = load_rows(keep, wq, "pooled_raw")
         w_raw = [load_rows(weight_rows, W_w[0:CHUNK_ROWS, :], "weight_raw")]
         u_raw.append(load_rows(weight_rows, U_w[CHUNK_ROWS:FEATURES, :], "weight_raw"))
         w_raw.append(load_rows(weight_rows, W_w[CHUNK_ROWS:FEATURES, :], "weight_raw"))
@@ -278,54 +282,70 @@ def tile_gatedmemorymodule_pb_t_kernel(tc, queries, memory_items, wq, U_w, W_w, 
         def difference(n):
             nc.vector.tensor_sub(out=step[:, n, :], in0=pooled_raw[:, n, :], in1=memory_raw[:, n, :])
 
+        sums = [{}, {}]
+        first_pair = range(0, TILES // 2)
+        second_pair = range(TILES // 2, TILES)
+
+        def start_sums(h, tiles):
+            for n in tiles:
+                total = sum_banks.tile([P, CHUNK_ROWS], F32, tag="total")
+                sums[h][n] = total
+                products(total, n, memory_mx, u_mx[h], True)
+
+        def finish_sums(h, tiles):
+            for n in tiles:
+                products(sums[h][n], n, pooled_mx, w_mx[h], False)
+
+        def blend_tiles(h, tiles):
+            for n in tiles:
+                blend(h, n, sums[h][n])
+
         roll(None, memory_chunk, False)
-        roll(memory_chunk, pooled_chunk, False)
+        roll(memory_chunk, u_chunk[0], False)
         quantise(memory_chunk)
-        difference(0)
-        roll(pooled_chunk, u_chunk[0], False)
-        quantise(pooled_chunk)
-        difference(1)
-        roll(u_chunk[0], w_chunk[0], False)
+        roll(u_chunk[0], pooled_chunk, False)
         quantise(u_chunk[0])
-        difference(2)
+        start_sums(0, first_pair)
+        roll(pooled_chunk, w_chunk[0], False)
+        quantise(pooled_chunk)
+        difference(0)
+        difference(1)
+        start_sums(0, second_pair)
         roll(w_chunk[0], u_chunk[1], False)
         quantise(w_chunk[0])
+        difference(2)
         difference(3)
+        finish_sums(0, first_pair)
         roll(u_chunk[1], w_chunk[1], False)
-        sums = []
-        for n in range(TILES):
-            total = sum_banks.tile([P, CHUNK_ROWS], F32, tag="total")
-            sums.append(total)
-            products(total, n, memory_mx, u_mx[0], True)
-        for n in range(TILES):
-            products(sums[n], n, pooled_mx, w_mx[0], False)
         quantise(u_chunk[1])
+        blend_tiles(0, first_pair)
+        finish_sums(0, second_pair)
         roll(w_chunk[1], query_chunk(0), False)
         refill(0)
         quantise(w_chunk[1])
-        next_sums = []
-        for n in range(TILES):
-            blend(0, n, sums[n])
-            total = sum_banks.tile([P, CHUNK_ROWS], F32, tag="total")
-            next_sums.append(total)
-            products(total, n, memory_mx, u_mx[1], True)
+        start_sums(1, first_pair)
+        blend_tiles(0, second_pair)
         store_slots(0)
-        for n in range(TILES):
-            products(next_sums[n], n, pooled_mx, w_mx[1], False)
-        roll(query_chunk(0), new_chunk[0], False)
-        quantise(query_chunk(0))
-        for n in range(TILES):
-            blend(1, n, next_sums[n])
+        roll(query_chunk(0), None, False)
+        finish_sums(1, first_pair)
+        start_sums(1, second_pair)
+        finish_sums(1, second_pair)
+        blend_tiles(1, first_pair)
+        roll(None, new_chunk[0], False)
+        blend_tiles(1, second_pair)
         store_slots(1)
+        quantise(query_chunk(0))
         roll(new_chunk[0], new_chunk[1], False)
         quantise(new_chunk[0])
+        begin_answer(0)
+        for n in range(TILES):
+            logit_pass(0, n, 0)
         roll(new_chunk[1], query_chunk(1), False)
         refill(1)
         quantise(new_chunk[1])
-
-        begin_answer(0)
         for n in range(TILES):
-            multiply(0, n)
+            logit_pass(0, n, 1)
+
         roll(query_chunk(1), query_chunk(2), False)
         refill(2)
         quantise(query_chunk(1))

from contextlib import ExitStack

import concourse.mybir as mybir
from concourse.masks import make_identity

F32 = mybir.dt.float32
BF16 = mybir.dt.bfloat16
U32 = mybir.dt.uint32
U8 = mybir.dt.uint8
FP8X4 = mybir.dt.float8_e4m3fn_x4
ACT = mybir.ActivationFunctionType
ALU = mybir.AluOpType

P = 128
FEATURES = 1024
SLOTS = 512
BATCH = 32
TEMPERATURE = 0.1
PACK = 4
K_PASS = P * PACK
PASSES = FEATURES // K_PASS
TILES = 4
CHUNK_ROWS = TILES * P
CHUNK_WORDS = CHUNK_ROWS * PASSES
HALVES = FEATURES // CHUNK_ROWS
QUERY_CHUNKS = BATCH // TILES
QUERY_BUFFERS = 4
STORE_TILES = 2

FLOPS = 2 * (2 * SLOTS * FEATURES * FEATURES) + 2 * (P * BATCH) * SLOTS * FEATURES


def stationary_cols(n, g):
    return slice((n * PASSES + g) * P, (n * PASSES + g + 1) * P)


def moving_cols(g):
    return slice(g * CHUNK_ROWS, (g + 1) * CHUNK_ROWS)


def in_tile_order(bank):
    return bank.rearrange("p (n r) -> p r n", n=TILES)


def in_row_order(row):
    return row.rearrange("p (r n) -> p r n", n=TILES)


def tile_gatedmemorymodule_pb_t_kernel(tc, queries, memory_items, wq, U_w, W_w, out_0, out_1):
    nc = tc.nc
    with ExitStack() as ctx:
        keep = ctx.enter_context(tc.tile_pool(name="keep", bufs=1))
        weight_rows = ctx.enter_context(tc.tile_pool(name="weight_rows", bufs=2 * HALVES))
        query_rows = ctx.enter_context(tc.tile_pool(name="query_rows", bufs=QUERY_BUFFERS))
        regroup = ctx.enter_context(tc.tile_pool(name="regroup", bufs=3))
        query_mx = ctx.enter_context(tc.tile_pool(name="query_mx", bufs=4))
        gates = ctx.enter_context(tc.tile_pool(name="gates", bufs=3))
        answers = ctx.enter_context(tc.tile_pool(name="answers", bufs=3))
        stats = ctx.enter_context(tc.tile_pool(name="stats", bufs=3))
        turn_banks = ctx.enter_context(tc.psum_pool(name="turn_banks", bufs=TILES))
        sum_banks = ctx.enter_context(tc.psum_pool(name="sum_banks", bufs=TILES))
        ctx.enter_context(tc.manual_schedule())

        identity = keep.tile([P, P], F32)
        make_identity(nc, identity[:])

        def load_rows(pool, rows, label):
            raw = pool.tile([P, TILES, FEATURES], BF16, name=label)
            nc.sync.dma_start(out=raw[:], in_=rows.rearrange("(p n) k -> p n k", n=TILES))
            return raw

        def load_queries(c):
            raw = query_rows.tile([P, TILES, FEATURES], BF16, name="query_raw")
            nc.sync.dma_start(out=raw[:], in_=queries[:, c * TILES : (c + 1) * TILES, :])
            return raw

        def new_operand(pool, label):
            codes = pool.tile([P, CHUNK_WORDS], U32, name=label + "_codes", align_bytes=64)
            scales = pool.tile([P, CHUNK_WORDS], U8, name=label + "_scales", align_bytes=64)
            return codes, scales

        def input_chunk(raw, operand, order):
            words = raw[:].bitcast(F32)
            return {
                "blocks": [[words[:, n, j * P : (j + 1) * P] for j in range(PACK)] for n in range(TILES)],
                "order": order,
                "codes": operand[0][:],
                "scales": operand[1][:],
                "banks": [],
            }

        def slots_chunk(g):
            blocks = []
            for n in range(TILES):
                by_code = new_slots[:, n, g * K_PASS : (g + 1) * K_PASS].rearrange(
                    "p (u q e) -> p u e q", u=2, e=2
                )
                blocks.append([by_code[:, t // 2, t % 2, :] for t in range(PACK)])
            return {
                "blocks": blocks,
                "order": None,
                "codes": new_mx[0][:, moving_cols(g)],
                "scales": new_mx[1][:, moving_cols(g)],
                "banks": [],
            }

        def turn(chunk, n):
            turned = turn_banks.tile([P, PACK, P], F32, tag="turned")
            for j in range(PACK):
                nc.tensor.transpose(turned[:, j, :], chunk["blocks"][n][j], identity[:])
            chunk["banks"].append(turned)

        def make_room(chunk):
            if chunk["order"] is None:
                grouped = regroup.tile([P, SLOTS * PACK], BF16, tag="grouped", align_bytes=64)
                chunk["targets"] = grouped[:].rearrange("p (n g r t) -> p n g r t", n=TILES, g=1, t=PACK)
                chunk["side_by_side"] = PACK
            else:
                grouped = regroup.tile([P, CHUNK_WORDS * PACK], BF16, tag="grouped", align_bytes=64)
                chunk["targets"] = grouped[:].bitcast(F32).rearrange(
                    "p (" + chunk["order"] + " u) -> p n g r u", n=TILES, g=PASSES, u=2
                )
                chunk["side_by_side"] = 2
            chunk["grouped"] = grouped

        def copy_out(chunk, n, engine_copy):
            engine_copy(
                out=chunk["targets"][:, n],
                in_=chunk["banks"][n][:].rearrange("p (g u) r -> p g r u", u=chunk["side_by_side"]),
            )

        def roll(leaving, entering, vector_helps):
            if leaving is not None:
                make_room(leaving)
            for n in range(TILES):
                if leaving is not None:
                    if vector_helps and n == TILES - 1:
                        copy_out(leaving, n, nc.vector.tensor_copy)
                    else:
                        copy_out(leaving, n, nc.scalar.copy)
                if entering is not None:
                    turn(entering, n)

        def quantise(chunk):
            nc.vector.quantize_mx(
                out=chunk["codes"].bitcast(FP8X4), scales=chunk["scales"], in_=chunk["grouped"][:]
            )

        def products(total, n, slot_mx, weight_mx, first):
            for g in range(PASSES):
                nc.tensor.matmul_mx(
                    out=total[:],
                    lhsT=slot_mx[0][:, stationary_cols(n, g)].bitcast(FP8X4),
                    lhsT_scale=slot_mx[1][:, stationary_cols(n, g)],
                    rhs=weight_mx[0][:, moving_cols(g)].bitcast(FP8X4),
                    rhs_scale=weight_mx[1][:, moving_cols(g)],
                    start=(first and g == 0),
                    stop=(not first and g == PASSES - 1),
                )

        def blend(h, n, total):
            cols = slice(h * CHUNK_ROWS, (h + 1) * CHUNK_ROWS)
            lift = gates.tile([P, CHUNK_ROWS], F32)
            nc.scalar.activation(out=in_row_order(lift[:]), in_=in_tile_order(total[:]), func=ACT.Tanh, scale=0.5)
            nc.vector.scalar_tensor_tensor(
                out=lift[:], in0=lift[:], scalar=1.0, in1=step[:, n, cols], op0=ALU.add, op1=ALU.mult
            )
            nc.vector.scalar_tensor_tensor(
                out=new_slots[:, n, cols], in0=lift[:], scalar=0.5, in1=memory_raw[:, n, cols],
                op0=ALU.mult, op1=ALU.add,
            )

        def store_slots(h):
            cols = slice(h * CHUNK_ROWS, (h + 1) * CHUNK_ROWS)
            nc.sync.dma_start(
                out=out_0.rearrange("(p n) k -> p n k", n=TILES)[:, :, cols], in_=new_slots[:, :, cols]
            )

        query_raw = {}
        query = {}

        def query_chunk(c):
            if c >= QUERY_CHUNKS:
                return None
            if c not in query:
                query[c] = input_chunk(query_raw[c], new_operand(query_mx, "query"), "n g r")
            return query[c]

        def refill(c):
            if c + QUERY_BUFFERS < QUERY_CHUNKS:
                query_raw[c + QUERY_BUFFERS] = load_queries(c + QUERY_BUFFERS)

        def begin_answer(c):
            answer = answers.tile([P, TILES, SLOTS], F32)
            shift = stats.tile([P, TILES], F32)
            row_sum = stats.tile([P, TILES], F32)
            inverse = stats.tile([P, TILES], F32)
            query[c]["answer"] = answer
            query[c]["shift"] = shift
            query[c]["row_sum"] = row_sum
            query[c]["inverse"] = inverse
            query[c]["sums"] = []

        def logit_pass(c, n, g):
            if g == 0:
                total = sum_banks.tile([P, SLOTS], F32, tag="total")
                query[c]["sums"].append(total)
            nc.tensor.matmul_mx(
                out=query[c]["sums"][n][:],
                lhsT=query[c]["codes"][:, stationary_cols(n, g)].bitcast(FP8X4),
                lhsT_scale=query[c]["scales"][:, stationary_cols(n, g)],
                rhs=new_mx[0][:, moving_cols(g)].bitcast(FP8X4),
                rhs_scale=new_mx[1][:, moving_cols(g)],
                start=(g == 0),
                stop=(g == PASSES - 1),
            )

        def multiply(c, n):
            for g in range(PASSES):
                logit_pass(c, n, g)

        def leave_bank(c, n):
            nc.vector.tensor_scalar(
                out=in_row_order(query[c]["answer"][:, n, :]),
                in0=in_tile_order(query[c]["sums"][n][:]),
                scalar1=-1.0 / TEMPERATURE,
                scalar2=None,
                op0=ALU.mult,
                op1=ALU.min,
                accum_out=query[c]["shift"][:, n : n + 1],
            )

        def exponential(c, n):
            nc.scalar.activation(
                out=query[c]["answer"][:, n, :],
                in_=query[c]["answer"][:, n, :],
                func=ACT.Exp,
                bias=query[c]["shift"][:, n : n + 1],
                scale=-1.0,
                accum_out=query[c]["row_sum"][:, n : n + 1],
            )

        def normalise(c):
            nc.vector.reciprocal(out=query[c]["inverse"][:], in_=query[c]["row_sum"][:])
            for n in range(TILES):
                row = query[c]["answer"][:, n, :]
                factor = query[c]["inverse"][:, n : n + 1]
                if c == QUERY_CHUNKS - 1:
                    nc.vector.tensor_scalar_mul(out=row, in0=row, scalar1=factor)
                else:
                    nc.gpsimd.tensor_scalar(
                        out=row, in0=row, scalar1=factor, scalar2=0.0, op0=ALU.mult, op1=ALU.add
                    )
                if (n + 1) % STORE_TILES == 0:
                    done = slice(n + 1 - STORE_TILES, n + 1)
                    entries = slice(c * TILES + n + 1 - STORE_TILES, c * TILES + n + 1)
                    nc.sync.dma_start(out=out_1[:, entries, :], in_=query[c]["answer"][:, done, :])

        memory_raw = load_rows(keep, memory_items, "memory_raw")
        u_raw = [load_rows(weight_rows, U_w[0:CHUNK_ROWS, :], "weight_raw")]
        pooled_raw = load_rows(keep, wq, "pooled_raw")
        w_raw = [load_rows(weight_rows, W_w[0:CHUNK_ROWS, :], "weight_raw")]
        u_raw.append(load_rows(weight_rows, U_w[CHUNK_ROWS:FEATURES, :], "weight_raw"))
        w_raw.append(load_rows(weight_rows, W_w[CHUNK_ROWS:FEATURES, :], "weight_raw"))
        for c in range(QUERY_BUFFERS):
            query_raw[c] = load_queries(c)

        memory_mx = new_operand(keep, "memory")
        pooled_mx = new_operand(keep, "pooled")
        u_mx = [new_operand(keep, "u%d" % h) for h in range(HALVES)]
        w_mx = [new_operand(keep, "w%d" % h) for h in range(HALVES)]
        new_mx = new_operand(keep, "new_slots")
        step = keep.tile([P, TILES, FEATURES], F32)
        new_slots = keep.tile([P, TILES, FEATURES], F32)

        memory_chunk = input_chunk(memory_raw, memory_mx, "n g r")
        pooled_chunk = input_chunk(pooled_raw, pooled_mx, "n g r")
        u_chunk = [input_chunk(u_raw[h], u_mx[h], "g n r") for h in range(HALVES)]
        w_chunk = [input_chunk(w_raw[h], w_mx[h], "g n r") for h in range(HALVES)]
        new_chunk = [slots_chunk(g) for g in range(PASSES)]

        def difference(n):
            nc.vector.tensor_sub(out=step[:, n, :], in0=pooled_raw[:, n, :], in1=memory_raw[:, n, :])

        sums = [{}, {}]
        first_pair = range(0, TILES // 2)
        second_pair = range(TILES // 2, TILES)

        def start_sums(h, tiles):
            for n in tiles:
                total = sum_banks.tile([P, CHUNK_ROWS], F32, tag="total")
                sums[h][n] = total
                products(total, n, memory_mx, u_mx[h], True)

        def finish_sums(h, tiles):
            for n in tiles:
                products(sums[h][n], n, pooled_mx, w_mx[h], False)

        def blend_tiles(h, tiles):
            for n in tiles:
                blend(h, n, sums[h][n])

        roll(None, memory_chunk, False)
        roll(memory_chunk, u_chunk[0], False)
        quantise(memory_chunk)
        roll(u_chunk[0], pooled_chunk, False)
        quantise(u_chunk[0])
        start_sums(0, first_pair)
        roll(pooled_chunk, w_chunk[0], False)
        quantise(pooled_chunk)
        difference(0)
        difference(1)
        start_sums(0, second_pair)
        roll(w_chunk[0], u_chunk[1], False)
        quantise(w_chunk[0])
        difference(2)
        difference(3)
        finish_sums(0, first_pair)
        roll(u_chunk[1], w_chunk[1], False)
        quantise(u_chunk[1])
        blend_tiles(0, first_pair)
        finish_sums(0, second_pair)
        roll(w_chunk[1], query_chunk(0), False)
        refill(0)
        quantise(w_chunk[1])
        start_sums(1, first_pair)
        blend_tiles(0, second_pair)
        store_slots(0)
        roll(query_chunk(0), None, False)
        finish_sums(1, first_pair)
        start_sums(1, second_pair)
        finish_sums(1, second_pair)
        blend_tiles(1, first_pair)
        roll(None, new_chunk[0], False)
        blend_tiles(1, second_pair)
        store_slots(1)
        quantise(query_chunk(0))
        roll(new_chunk[0], new_chunk[1], False)
        quantise(new_chunk[0])
        begin_answer(0)
        for n in range(TILES):
            logit_pass(0, n, 0)
        roll(new_chunk[1], query_chunk(1), False)
        refill(1)
        quantise(new_chunk[1])
        for n in range(TILES):
            logit_pass(0, n, 1)

        roll(query_chunk(1), query_chunk(2), False)
        refill(2)
        quantise(query_chunk(1))
        roll(query_chunk(2), query_chunk(3), False)
        refill(3)
        for c in range(QUERY_CHUNKS):
            if c + 1 < QUERY_CHUNKS:
                begin_answer(c + 1)
            for n in range(TILES):
                leave_bank(c, n)
                if c + 1 < QUERY_CHUNKS:
                    multiply(c + 1, n)
                exponential(c, n)
            if c + 3 < QUERY_CHUNKS:
                roll(query_chunk(c + 3), query_chunk(c + 4), True)
                refill(c + 4)
            if c + 2 < QUERY_CHUNKS:
                quantise(query_chunk(c + 2))
            normalise(c)
